import numpy as np
import ml_dtypes


def mxq(x, axis, fmt="e4m3"):
    dtype, down = {"e4m3": (ml_dtypes.float8_e4m3fn, 7), "e5m2": (ml_dtypes.float8_e5m2, 14)}[fmt]
    v = np.moveaxis(np.asarray(x, np.float32).astype(ml_dtypes.bfloat16).astype(np.float64), axis, -1)
    blocks = v.reshape(v.shape[:-1] + (-1, 32))
    amax = np.abs(blocks).max(-1, keepdims=True)
    byte = np.maximum(np.where(amax > 0, np.frexp(amax)[1] - 1 + 127, 0) - down, 1)
    scale = np.exp2(byte - 127.0)
    codes = (blocks / scale).astype(np.float32).astype(dtype).astype(np.float64)
    return np.moveaxis((codes * scale).reshape(v.shape), -1, axis)


WIDE = False


def mx_kscale(k):
    if not WIDE:
        return np.ones(k)
    levels = np.array([10, -10, 5, -5, 0])
    a = np.random.permutation(np.resize(levels, k // 512 * 4)).reshape(k // 512, 4)
    idx = np.arange(k)
    return np.exp2(a[idx // 512, idx % 128 // 32])


BF16 = ml_dtypes.bfloat16


def bf(x):
    return np.asarray(x, np.float32).astype(BF16)


def f64(x):
    return np.asarray(x).astype(np.float64)


E2M1 = np.array([0.0, 0.5, 1.0, 1.5, 2.0, 3.0, 4.0, 6.0, -0.0, -0.5, -1.0, -1.5, -2.0, -3.0, -4.0, -6.0])


def pack_weight(w, fmt):
    k, n = w.shape
    w = f64(bf(w)).reshape(k // 32, 32, n)
    amax = np.abs(w).max(1)
    if fmt == "e4m3":
        byte = np.frexp(amax)[1] - 1 + 127 - 7
    else:
        mant, ex = np.frexp(amax / 6.0)
        byte = np.where(mant > 0.5, ex, ex - 1) + 127
    byte = np.clip(np.where(amax > 0, byte, 1), 1, 254)
    scaled = (w * np.exp2(127.0 - byte)[:, None, :]).reshape(k, n).astype(np.float32)
    by_word = np.ascontiguousarray(scaled.reshape(k // 512, 128, 4, n).transpose(0, 1, 3, 2))
    if fmt == "e4m3":
        words = by_word.astype(ml_dtypes.float8_e4m3fn).view(np.uint8)
    else:
        c = by_word.astype(ml_dtypes.float4_e2m1fn).view(np.uint8) & 0xF
        words = c[..., 0::2] | (c[..., 1::2] << 4)
    return np.ascontiguousarray(words), np.ascontiguousarray(byte.astype(np.uint8).reshape(k // 512, 16, n))


def unpack_weight(words, scales, fmt):
    g, p, n, _ = words.shape
    if fmt == "e4m3":
        vals = np.ascontiguousarray(words).view(ml_dtypes.float8_e4m3fn).astype(np.float64)
    else:
        nib = np.empty((g, p, n, 4), np.uint8)
        nib[..., 0::2] = words & 0xF
        nib[..., 1::2] = words >> 4
        vals = E2M1[nib]
    vals = vals * np.repeat(np.exp2(scales.astype(np.float64) - 127.0), 8, axis=1)[..., None]
    return vals.transpose(0, 1, 3, 2).reshape(g * 512, n)

def pack4(w):
    words, scales = pack_weight(w, "e2m1")
    return words.reshape(words.shape[0], 128, -1), scales


def unpack4(words, scales):
    return unpack_weight(words.reshape(words.shape[0], 128, -1, 2), scales, "e2m1")


B, N, AB, MAXN, BB, H = 2, 16, 4192, 255, 32, 1024
TAIL = AB - (MAXN + 1)
AF = AB + TAIL
FB = AF + BB + BB


def setup_inputs():
    s = mx_kscale(FB)
    sa, sb = s[:AB], s[AF:AF + BB]
    se = np.concatenate([sa, sa[MAXN + 1:], sb, sb])
    f_atoms = bf(np.random.standard_normal((B, N, AB)) * sa)
    f_bonds = bf(np.random.standard_normal((B, N, N, BB)) * sb)
    adj = bf(np.random.uniform(size=(B, N, N)) * 4.0 / N)
    w = np.random.standard_normal((H, FB)) * 0.1 * N / np.sqrt(FB) / se
    words, scales = pack4(np.ascontiguousarray(w.T))
    return {"f_atoms": f_atoms,
            "f_bonds": f_bonds,
            "adj": adj,
            "W_i_w_words": words,
            "W_i_w_scales": scales}


def reference(f_atoms, f_bonds, adj, W_i_w_words, W_i_w_scales):
    f_atoms, f_bonds, adj = f64(f_atoms), f64(f_bonds), f64(adj)
    fa = np.concatenate([f_atoms, f_atoms[:, :, MAXN + 1:]], axis=-1)
    fa_exp = np.broadcast_to(fa[:, :, None, :], (B, N, N, AF))
    fb = np.concatenate([fa_exp, f_bonds, f_bonds], axis=-1)
    return mxq(adj[..., None] * fb, 3, "e4m3") @ unpack4(W_i_w_words, W_i_w_scales)

@@ -1,0 +1,260 @@
+from contextlib import ExitStack
+
+import concourse.mybir as mybir
+from concourse.masks import make_identity
+
+BF16 = mybir.dt.bfloat16
+F32 = mybir.dt.float32
+I32 = mybir.dt.int32
+U8 = mybir.dt.uint8
+U32 = mybir.dt.uint32
+FP8X4 = mybir.dt.float8_e4m3fn_x4
+FP4X4 = mybir.dt.float4_e2m1fn_x4
+MULT = mybir.AluOpType.mult
+
+P = 128
+PACK = 4
+K_PASS = P * PACK
+BLOCK = 32
+BLOCK_PARTS = BLOCK // PACK
+PASS_BLOCKS = K_PASS // BLOCK
+
+ATOMS = 16
+SOURCES = 32
+PAIRS = SOURCES * ATOMS
+ATOM_FEATS = 4192
+ONCE_FEATS = 256
+BOND_FEATS = 32
+H = 1024
+
+FULL_TILES = ATOM_FEATS // K_PASS
+LAST = FULL_TILES
+REST_FEATS = ATOM_FEATS - FULL_TILES * K_PASS
+COPY_SHIFT = (ATOM_FEATS - ONCE_FEATS) // BLOCK
+
+PAIR_TILES = PAIRS // P
+SOURCES_PER_TILE = P // ATOMS
+N_COLS = 512
+COL_TILES = H // N_COLS
+
+X_CHUNKS = P // SOURCES
+X_FEATS = FULL_TILES * K_PASS // X_CHUNKS
+X_TILES = X_FEATS // K_PASS
+
+TILES_PER_SCALE_RUN = 4
+SWEPT_TILES = 7
+
+FLOPS = 2 * PAIRS * (2 * ATOM_FEATS - ONCE_FEATS + 2 * BOND_FEATS) * H
+
+
+def tile_mpnencoder_pa_k_kernel(tc, f_atoms, f_bonds, adj, W_i_w_words, W_i_w_scales, out):
+    nc = tc.nc
+    word_rows = W_i_w_words.rearrange("g p n -> (g p) n")
+    scale_rows = W_i_w_scales.rearrange("g q n -> (g q) n")
+    out_rows = out.rearrange("b m n h -> (b m n) h")
+
+    with ExitStack() as ctx:
+        ctx.enter_context(tc.manual_schedule())
+        keep = ctx.enter_context(tc.tile_pool(name="keep", bufs=1))
+        stage = ctx.enter_context(tc.tile_pool(name="stage", bufs=3))
+        results = ctx.enter_context(tc.tile_pool(name="results", bufs=4))
+        psum = ctx.enter_context(tc.psum_pool(name="psum", bufs=1))
+
+        first_words = keep.tile([P, FULL_TILES, 2 * H], U8, align_bytes=64)
+        second_words = keep.tile([P, FULL_TILES, 2 * H], U8, align_bytes=64)
+        last_words = keep.tile([P, 2 * H], U8, align_bytes=64)
+        first_planes = keep.tile([P, FULL_TILES, H], U8, align_bytes=64)
+        second_planes = keep.tile([P, FULL_TILES, H], U8, align_bytes=64)
+        last_plane = keep.tile([P, H], U8, align_bytes=64)
+        g_codes = keep.tile([P, FULL_TILES + 1, PAIRS], U32, align_bytes=64)
+        g_planes = keep.tile([P, FULL_TILES + 1, PAIRS], U8, align_bytes=64)
+
+        identity = keep.tile([P, P], F32)
+        ones = keep.tile([P, P], BF16)
+        adj_row = keep.tile([P, PAIRS], BF16)
+        adj_x4 = keep.tile([P, PAIRS, PACK], BF16)
+        x_sb = keep.tile([P, X_FEATS], BF16)
+        atoms_t = keep.tile([P, FULL_TILES + 1, SOURCES, PACK], BF16)
+        bonds_t = keep.tile([2 * BLOCK_PARTS, PAIRS, PACK], BF16)
+
+        nc.gpsimd.memset(ones[:], 1.0)
+        make_identity(nc, identity[:])
+        nc.vector.memset(adj_row[:], 0.0)
+        nc.vector.memset(atoms_t[0 : 2 * BLOCK_PARTS, LAST, :, :], 0.0)
+
+        nc.scalar.dma_start(out=adj_row[0:1, :], in_=adj.rearrange("b m n -> (b m n)").unsqueeze(0))
+        nc.scalar.dma_start(
+            out=x_sb[:],
+            in_=f_atoms[:, :, 0 : X_CHUNKS * X_FEATS].rearrange("b m (c j) -> (b m) c j", c=X_CHUNKS),
+        )
+
+        def load_words(words, first_block, blocks, first_part):
+            nc.sync.dma_start(
+                out=words[first_part : first_part + BLOCK_PARTS * blocks, :].bitcast(I32),
+                in_=word_rows[BLOCK_PARTS * first_block : BLOCK_PARTS * (first_block + blocks), :].bitcast(I32),
+            )
+
+        def load_planes(planes, first_block):
+            count = planes.shape[1]
+            nc.vector.memset(planes.bitcast(I32), 0)
+            rows = scale_rows[first_block : first_block + PASS_BLOCKS * count, :].rearrange(
+                "(i q s) n -> s q i n", q=4, s=4
+            )
+            for s in range(4):
+                nc.sync.dma_start(out=planes[s:P:32, :, :].bitcast(I32), in_=rows[s].bitcast(I32))
+
+        for i in range(FULL_TILES):
+            load_words(first_words[:, i, :], PASS_BLOCKS * i, PASS_BLOCKS, 0)
+            if i > 0:
+                load_words(second_words[:, i, :], PASS_BLOCKS * i + COPY_SHIFT, PASS_BLOCKS, 0)
+            if i % TILES_PER_SCALE_RUN == 0:
+                end = i + TILES_PER_SCALE_RUN
+                load_planes(first_planes[:, i:end, :], PASS_BLOCKS * i)
+                begin = max(i, 1)
+                load_planes(second_planes[:, begin:end, :], PASS_BLOCKS * begin + COPY_SHIFT)
+
+        rest_blocks = REST_FEATS // BLOCK
+        once_blocks = ONCE_FEATS // BLOCK
+        atom_blocks = ATOM_FEATS // BLOCK
+        bond_run = (0, atom_blocks + COPY_SHIFT, 2)
+        rest_first_run = (2, FULL_TILES * PASS_BLOCKS, rest_blocks)
+        low_second_run = (2 + rest_blocks, atom_blocks, PASS_BLOCKS - once_blocks)
+        rest_second_run = (PASS_BLOCKS - rest_blocks, FULL_TILES * PASS_BLOCKS + COPY_SHIFT, rest_blocks)
+        nc.vector.memset(last_plane[:].bitcast(I32), 0)
+        for position, first_block, blocks in (bond_run, rest_first_run, low_second_run, rest_second_run):
+            load_words(last_words[:], first_block, blocks, BLOCK_PARTS * position)
+            done = 0
+            while done < blocks:
+                q = position + done
+                step = min(4 - q % 4, blocks - done)
+                part = 32 * (q // 4) + q % 4
+                nc.sync.dma_start(
+                    out=last_plane[part : part + step, :].bitcast(I32),
+                    in_=scale_rows[first_block + done : first_block + done + step, :].bitcast(I32),
+                )
+                done += step
+
+        adj_ps = psum.tile([P, PAIRS], F32, tag="bank6")
+        xt = psum.tile([P, X_TILES, 2, P], F32, tag="bank7")
+        nc.tensor.matmul(out=adj_ps[:], lhsT=ones[:], rhs=adj_row[:], start=True, stop=True)
+        x_words = x_sb[:].bitcast(F32)
+        words_per_tile = K_PASS // 2
+        for l in range(X_TILES):
+            for u in range(2):
+                nc.tensor.transpose(
+                    xt[:, l, u, :],
+                    x_words[:, words_per_tile * l + u : words_per_tile * (l + 1) : 2],
+                    identity[:],
+                )
+        atoms_words = atoms_t[:].bitcast(F32)
+
+        def atoms_out_of_psum(copy, l):
+            copy(
+                out=atoms_words[:, l:FULL_TILES:X_TILES, :, :],
+                in_=xt[:, l, :, :].rearrange("p u (a c) -> p c a u", c=X_CHUNKS),
+            )
+
+        atoms_out_of_psum(nc.vector.tensor_copy, 0)
+        for r in range(PAIR_TILES):
+            pairs = slice(P * r, P * (r + 1))
+            nc.scalar.copy(
+                out=adj_x4[:, pairs, :],
+                in_=adj_ps[:, pairs].unsqueeze(2).to_broadcast([P, P, PACK]),
+            )
+        atoms_out_of_psum(nc.scalar.copy, 1)
+
+        with nc.allow_non_contiguous_dma(reason="runs of four features, needed late"):
+            for position, first_feat, blocks in (
+                (rest_first_run[0], FULL_TILES * K_PASS, rest_blocks),
+                (low_second_run[0], ONCE_FEATS, PASS_BLOCKS - once_blocks),
+                (rest_second_run[0], FULL_TILES * K_PASS, rest_blocks),
+            ):
+                nc.scalar.dma_start(
+                    out=atoms_t[BLOCK_PARTS * position : BLOCK_PARTS * (position + blocks), LAST, :, :],
+                    in_=f_atoms[:, :, first_feat : first_feat + BLOCK * blocks].rearrange(
+                        "b m (p t) -> p (b m) t", t=PACK
+                    ),
+                )
+            for copy_index in range(2):
+                nc.scalar.dma_start(
+                    out=bonds_t[BLOCK_PARTS * copy_index : BLOCK_PARTS * (copy_index + 1), :, :],
+                    in_=f_bonds.rearrange("b m n (p t) -> p (b m n) t", t=PACK),
+                )
+
+        def gate(i, r):
+            pairs = slice(P * r, P * (r + 1))
+            grouped = stage.tile([P, P, PACK], BF16, align_bytes=64, name="grouped")
+            nc.vector.tensor_tensor(
+                out=grouped[:].rearrange("p (a n) t -> p a n t", n=ATOMS),
+                in0=atoms_t[:, i, SOURCES_PER_TILE * r : SOURCES_PER_TILE * (r + 1), :]
+                .unsqueeze(2)
+                .to_broadcast([P, SOURCES_PER_TILE, ATOMS, PACK]),
+                in1=adj_x4[:, pairs, :].rearrange("p (a n) t -> p a n t", n=ATOMS),
+                op=MULT,
+            )
+            if i == LAST:
+                bond_parts = slice(0, 2 * BLOCK_PARTS)
+                nc.vector.tensor_tensor(
+                    out=grouped[bond_parts, :, :],
+                    in0=bonds_t[:, pairs, :],
+                    in1=adj_x4[bond_parts, pairs, :],
+                    op=MULT,
+                )
+            return grouped
+
+        def quantise(i, r, grouped):
+            pairs = slice(P * r, P * (r + 1))
+            nc.vector.quantize_mx(
+                out=g_codes[:, i, pairs].bitcast(FP8X4),
+                scales=g_planes[:, i, pairs],
+                in_=grouped[:].rearrange("p w t -> p (w t)"),
+            )
+
+        partners = [[(first_words[:, i, :], first_planes[:, i, :])] for i in range(FULL_TILES)]
+        for i in range(1, FULL_TILES):
+            partners[i].append((second_words[:, i, :], second_planes[:, i, :]))
+        partners.append([(last_words[:], last_plane[:])])
+
+        banks = {}
+        for r in range(PAIR_TILES):
+            for c in range(COL_TILES):
+                banks[(r, c)] = psum.tile(
+                    [P, N_COLS], F32, name="bank%d" % (COL_TILES * r + c), tag="bank%d" % (COL_TILES * r + c)
+                )
+
+        def mx_passes(i, r, c):
+            pairs = slice(P * r, P * (r + 1))
+            for words, plane in partners[i]:
+                nc.tensor.matmul_mx(
+                    out=banks[(r, c)][:],
+                    lhsT=g_codes[:, i, pairs].bitcast(FP8X4),
+                    lhsT_scale=g_planes[:, i, pairs],
+                    rhs=words[:, 2 * N_COLS * c : 2 * N_COLS * (c + 1)].bitcast(FP4X4),
+                    rhs_scale=plane[:, N_COLS * c : N_COLS * (c + 1)],
+                    start=(i == 0),
+                    stop=(i == LAST),
+                )
+
+        steps = [(i, r) for i in range(FULL_TILES + 1) for r in range(PAIR_TILES)]
+        gated = gate(*steps[0])
+        for index, (i, r) in enumerate(steps):
+            ready = gated
+            if index + 1 < len(steps):
+                gated = gate(*steps[index + 1])
+            quantise(i, r, ready)
+            if i < SWEPT_TILES:
+                for c in range(COL_TILES):
+                    mx_passes(i, r, c)
+
+        for r in range(PAIR_TILES):
+            for c in range(COL_TILES):
+                for i in range(SWEPT_TILES, FULL_TILES + 1):
+                    mx_passes(i, r, c)
+                result = results.tile([P, N_COLS], F32, name="result")
+                if c % 2 == 0:
+                    nc.scalar.copy(out=result[:], in_=banks[(r, c)][:])
+                else:
+                    nc.vector.tensor_copy(out=result[:], in_=banks[(r, c)][:])
+                nc.sync.dma_start(
+                    out=out_rows[P * r : P * (r + 1), N_COLS * c : N_COLS * (c + 1)], in_=result[:]
+                )

@@ -42,7 +42,12 @@ X_FEATS = FULL_TILES * K_PASS // X_CHUNKS
 X_TILES = X_FEATS // K_PASS
 
 TILES_PER_SCALE_RUN = 4
-SWEPT_TILES = 7
+EARLY_PAIR_TILES = PAIR_TILES - 1
+TRANSPOSE_LAST_BEFORE = 2
+
+def bank_name(r, c):
+    return "bank%d" % (COL_TILES * r + c)
+
 
 FLOPS = 2 * PAIRS * (2 * ATOM_FEATS - ONCE_FEATS + 2 * BOND_FEATS) * H
 
@@ -76,11 +81,12 @@ def tile_mpnencoder_pa_k_kernel(tc, f_atoms, f_bonds, adj, W_i_w_words, W_i_w_sc
         x_sb = keep.tile([P, X_FEATS], BF16)
         atoms_t = keep.tile([P, FULL_TILES + 1, SOURCES, PACK], BF16)
         bonds_t = keep.tile([2 * BLOCK_PARTS, PAIRS, PACK], BF16)
+        z_sb = keep.tile([P, PAIR_TILES, K_PASS], BF16)
 
         nc.gpsimd.memset(ones[:], 1.0)
         make_identity(nc, identity[:])
         nc.vector.memset(adj_row[:], 0.0)
-        nc.vector.memset(atoms_t[0 : 2 * BLOCK_PARTS, LAST, :, :], 0.0)
+        nc.gpsimd.memset(z_sb[:], 0.0)
 
         nc.scalar.dma_start(out=adj_row[0:1, :], in_=adj.rearrange("b m n -> (b m n)").unsqueeze(0))
         nc.scalar.dma_start(
@@ -134,8 +140,8 @@ def tile_mpnencoder_pa_k_kernel(tc, f_atoms, f_bonds, adj, W_i_w_words, W_i_w_sc
                 )
                 done += step
 
-        adj_ps = psum.tile([P, PAIRS], F32, tag="bank6")
-        xt = psum.tile([P, X_TILES, 2, P], F32, tag="bank7")
+        adj_ps = psum.tile([P, PAIRS], F32, tag=bank_name(EARLY_PAIR_TILES, 0))
+        xt = psum.tile([P, X_TILES, 2, P], F32, tag=bank_name(EARLY_PAIR_TILES, 1))
         nc.tensor.matmul(out=adj_ps[:], lhsT=ones[:], rhs=adj_row[:], start=True, stop=True)
         x_words = x_sb[:].bitcast(F32)
         words_per_tile = K_PASS // 2
@@ -163,23 +169,42 @@ def tile_mpnencoder_pa_k_kernel(tc, f_atoms, f_bonds, adj, W_i_w_words, W_i_w_sc
             )
         atoms_out_of_psum(nc.scalar.copy, 1)
 
-        with nc.allow_non_contiguous_dma(reason="runs of four features, needed late"):
-            for position, first_feat, blocks in (
-                (rest_first_run[0], FULL_TILES * K_PASS, rest_blocks),
-                (low_second_run[0], ONCE_FEATS, PASS_BLOCKS - once_blocks),
-                (rest_second_run[0], FULL_TILES * K_PASS, rest_blocks),
-            ):
-                nc.scalar.dma_start(
-                    out=atoms_t[BLOCK_PARTS * position : BLOCK_PARTS * (position + blocks), LAST, :, :],
-                    in_=f_atoms[:, :, first_feat : first_feat + BLOCK * blocks].rearrange(
-                        "b m (p t) -> p (b m) t", t=PACK
+        bond_rows = f_bonds.rearrange("b m n f -> (b m n) f").rearrange("(s j) f -> j s f", j=P)
+        for position in range(bond_run[0], bond_run[0] + bond_run[2]):
+            nc.scalar.dma_start(out=z_sb[:, :, BLOCK * position : BLOCK * (position + 1)], in_=bond_rows)
+        for position, first_feat, blocks in (
+            (rest_first_run[0], FULL_TILES * K_PASS, rest_blocks),
+            (low_second_run[0], ONCE_FEATS, PASS_BLOCKS - once_blocks),
+            (rest_second_run[0], FULL_TILES * K_PASS, rest_blocks),
+        ):
+            nc.scalar.dma_start(
+                out=z_sb[0:SOURCES, 0, BLOCK * position : BLOCK * (position + blocks)],
+                in_=f_atoms[:, :, first_feat : first_feat + BLOCK * blocks].rearrange("b m j -> (b m) j"),
+            )
+
+        def transpose_last_tile():
+            z_words = z_sb[:].bitcast(F32)
+            bonds_words = bonds_t[:].bitcast(F32)
+            bond_parts = slice(0, 2 * BLOCK_PARTS)
+            slabs_per_bank = N_COLS // (2 * P)
+            for half in range(PAIR_TILES // slabs_per_bank):
+                zt = psum.tile([P, slabs_per_bank, 2, P], F32, name="zt", tag=bank_name(EARLY_PAIR_TILES, half))
+                for s in range(slabs_per_bank):
+                    for u in range(2):
+                        nc.tensor.transpose(
+                            zt[:, s, u, :], z_words[:, slabs_per_bank * half + s, u : K_PASS // 2 : 2], identity[:]
+                        )
+                nc.scalar.copy(
+                    out=bonds_words[:, slabs_per_bank * P * half : slabs_per_bank * P * (half + 1), :].rearrange(
+                        "p (s j) u -> p s j u", j=P
                     ),
+                    in_=zt[bond_parts, :, :, :].rearrange("p s u j -> p s j u"),
                 )
-            for copy_index in range(2):
-                nc.scalar.dma_start(
-                    out=bonds_t[BLOCK_PARTS * copy_index : BLOCK_PARTS * (copy_index + 1), :, :],
-                    in_=f_bonds.rearrange("b m n (p t) -> p (b m n) t", t=PACK),
-                )
+                if half == 0:
+                    nc.scalar.copy(
+                        out=atoms_words[:, LAST, :, :],
+                        in_=zt[:, 0, :, 0:SOURCES].rearrange("p u a -> p a u"),
+                    )
 
         def gate(i, r):
             pairs = slice(P * r, P * (r + 1))
@@ -216,11 +241,10 @@ def tile_mpnencoder_pa_k_kernel(tc, f_atoms, f_bonds, adj, W_i_w_words, W_i_w_sc
         partners.append([(last_words[:], last_plane[:])])
 
         banks = {}
-        for r in range(PAIR_TILES):
+
+        def open_banks(r):
             for c in range(COL_TILES):
-                banks[(r, c)] = psum.tile(
-                    [P, N_COLS], F32, name="bank%d" % (COL_TILES * r + c), tag="bank%d" % (COL_TILES * r + c)
-                )
+                banks[(r, c)] = psum.tile([P, N_COLS], F32, name=bank_name(r, c), tag=bank_name(r, c))
 
         def mx_passes(i, r, c):
             pairs = slice(P * r, P * (r + 1))
@@ -235,26 +259,37 @@ def tile_mpnencoder_pa_k_kernel(tc, f_atoms, f_bonds, adj, W_i_w_words, W_i_w_sc
                     stop=(i == LAST),
                 )
 
-        steps = [(i, r) for i in range(FULL_TILES + 1) for r in range(PAIR_TILES)]
+        def store_bank(r, c):
+            result = results.tile([P, N_COLS], F32, name="result")
+            if c % 2 == 0:
+                nc.scalar.copy(out=result[:], in_=banks[(r, c)][:])
+            else:
+                nc.vector.tensor_copy(out=result[:], in_=banks[(r, c)][:])
+            nc.sync.dma_start(out=out_rows[P * r : P * (r + 1), N_COLS * c : N_COLS * (c + 1)], in_=result[:])
+
+        for r in range(EARLY_PAIR_TILES):
+            open_banks(r)
+        tiles = range(FULL_TILES + 1)
+        steps = [(i, r) for i in tiles for r in range(EARLY_PAIR_TILES)]
+        steps.extend([(i, r) for r in range(EARLY_PAIR_TILES, PAIR_TILES) for i in tiles])
         gated = gate(*steps[0])
         for index, (i, r) in enumerate(steps):
+            if (i, r) == (TRANSPOSE_LAST_BEFORE, 0):
+                transpose_last_tile()
             ready = gated
             if index + 1 < len(steps):
                 gated = gate(*steps[index + 1])
             quantise(i, r, ready)
-            if i < SWEPT_TILES:
+            if r < EARLY_PAIR_TILES:
                 for c in range(COL_TILES):
                     mx_passes(i, r, c)
 
-        for r in range(PAIR_TILES):
+        for r in range(EARLY_PAIR_TILES):
             for c in range(COL_TILES):
-                for i in range(SWEPT_TILES, FULL_TILES + 1):
+                store_bank(r, c)
+        for r in range(EARLY_PAIR_TILES, PAIR_TILES):
+            open_banks(r)
+            for c in range(COL_TILES):
+                for i in tiles:
                     mx_passes(i, r, c)
-                result = results.tile([P, N_COLS], F32, name="result")
-                if c % 2 == 0:
-                    nc.scalar.copy(out=result[:], in_=banks[(r, c)][:])
-                else:
-                    nc.vector.tensor_copy(out=result[:], in_=banks[(r, c)][:])
-                nc.sync.dma_start(
-                    out=out_rows[P * r : P * (r + 1), N_COLS * c : N_COLS * (c + 1)], in_=result[:]
-                )
+                store_bank(r, c)

@@ -109,7 +109,31 @@ def tile_mpnencoder_pa_k_kernel(tc, f_atoms, f_bonds, adj, W_i_w_words, W_i_w_sc
             for s in range(4):
                 nc.sync.dma_start(out=planes[s:P:32, :, :].bitcast(I32), in_=rows[s].bitcast(I32))
 
+        rest_blocks = REST_FEATS // BLOCK
+        once_blocks = ONCE_FEATS // BLOCK
+        atom_blocks = ATOM_FEATS // BLOCK
+        bond_run = (0, atom_blocks + COPY_SHIFT, 2)
+        rest_first_run = (2, FULL_TILES * PASS_BLOCKS, rest_blocks)
+        low_second_run = (2 + rest_blocks, atom_blocks, PASS_BLOCKS - once_blocks)
+        rest_second_run = (PASS_BLOCKS - rest_blocks, FULL_TILES * PASS_BLOCKS + COPY_SHIFT, rest_blocks)
+
+        def load_last_tile_features():
+            bond_rows = f_bonds.rearrange("b m n f -> (b m n) f").rearrange("(s j) f -> j s f", j=P)
+            for position in range(bond_run[0], bond_run[0] + bond_run[2]):
+                nc.sync.dma_start(out=z_sb[:, :, BLOCK * position : BLOCK * (position + 1)], in_=bond_rows)
+            for position, first_feat, blocks in (
+                (rest_first_run[0], FULL_TILES * K_PASS, rest_blocks),
+                (low_second_run[0], ONCE_FEATS, PASS_BLOCKS - once_blocks),
+                (rest_second_run[0], FULL_TILES * K_PASS, rest_blocks),
+            ):
+                nc.sync.dma_start(
+                    out=z_sb[0:SOURCES, 0, BLOCK * position : BLOCK * (position + blocks)],
+                    in_=f_atoms[:, :, first_feat : first_feat + BLOCK * blocks].rearrange("b m j -> (b m) j"),
+                )
+
         for i in range(FULL_TILES):
+            if i == TRANSPOSE_LAST_BEFORE:
+                load_last_tile_features()
             load_words(first_words[:, i, :], PASS_BLOCKS * i, PASS_BLOCKS, 0)
             if i > 0:
                 load_words(second_words[:, i, :], PASS_BLOCKS * i + COPY_SHIFT, PASS_BLOCKS, 0)
@@ -119,13 +143,6 @@ def tile_mpnencoder_pa_k_kernel(tc, f_atoms, f_bonds, adj, W_i_w_words, W_i_w_sc
                 begin = max(i, 1)
                 load_planes(second_planes[:, begin:end, :], PASS_BLOCKS * begin + COPY_SHIFT)
 
-        rest_blocks = REST_FEATS // BLOCK
-        once_blocks = ONCE_FEATS // BLOCK
-        atom_blocks = ATOM_FEATS // BLOCK
-        bond_run = (0, atom_blocks + COPY_SHIFT, 2)
-        rest_first_run = (2, FULL_TILES * PASS_BLOCKS, rest_blocks)
-        low_second_run = (2 + rest_blocks, atom_blocks, PASS_BLOCKS - once_blocks)
-        rest_second_run = (PASS_BLOCKS - rest_blocks, FULL_TILES * PASS_BLOCKS + COPY_SHIFT, rest_blocks)
         nc.vector.memset(last_plane[:].bitcast(I32), 0)
         for position, first_block, blocks in (bond_run, rest_first_run, low_second_run, rest_second_run):
             load_words(last_words[:], first_block, blocks, BLOCK_PARTS * position)
@@ -168,19 +185,6 @@ def tile_mpnencoder_pa_k_kernel(tc, f_atoms, f_bonds, adj, W_i_w_words, W_i_w_sc
                 in_=adj_ps[:, pairs].unsqueeze(2).to_broadcast([P, P, PACK]),
             )
         atoms_out_of_psum(nc.scalar.copy, 1)
-
-        bond_rows = f_bonds.rearrange("b m n f -> (b m n) f").rearrange("(s j) f -> j s f", j=P)
-        for position in range(bond_run[0], bond_run[0] + bond_run[2]):
-            nc.scalar.dma_start(out=z_sb[:, :, BLOCK * position : BLOCK * (position + 1)], in_=bond_rows)
-        for position, first_feat, blocks in (
-            (rest_first_run[0], FULL_TILES * K_PASS, rest_blocks),
-            (low_second_run[0], ONCE_FEATS, PASS_BLOCKS - once_blocks),
-            (rest_second_run[0], FULL_TILES * K_PASS, rest_blocks),
-        ):
-            nc.scalar.dma_start(
-                out=z_sb[0:SOURCES, 0, BLOCK * position : BLOCK * (position + blocks)],
-                in_=f_atoms[:, :, first_feat : first_feat + BLOCK * blocks].rearrange("b m j -> (b m) j"),
-            )
 
         def transpose_last_tile():
             z_words = z_sb[:].bitcast(F32)

@@ -65,11 +65,22 @@ def tile_mpnencoder_pa_k_kernel(tc, f_atoms, f_bonds, adj, W_i_w_words, W_i_w_sc
         results = ctx.enter_context(tc.tile_pool(name="results", bufs=4))
         psum = ctx.enter_context(tc.psum_pool(name="psum", bufs=1))
 
-        first_words = keep.tile([P, FULL_TILES, 2 * H], U8, align_bytes=64)
-        second_words = keep.tile([P, FULL_TILES, 2 * H], U8, align_bytes=64)
+        first_words = {}
+        second_words = {}
+        for i in range(FULL_TILES):
+            first_words[i] = keep.tile([P, 2 * H], U8, align_bytes=64, name="first_words%d" % i)
+            if i > 0:
+                second_words[i] = keep.tile([P, 2 * H], U8, align_bytes=64, name="second_words%d" % i)
         last_words = keep.tile([P, 2 * H], U8, align_bytes=64)
-        first_planes = keep.tile([P, FULL_TILES, H], U8, align_bytes=64)
-        second_planes = keep.tile([P, FULL_TILES, H], U8, align_bytes=64)
+        first_planes = {}
+        second_planes = {}
+        for run in range(FULL_TILES // TILES_PER_SCALE_RUN):
+            first_planes[run] = keep.tile(
+                [P, TILES_PER_SCALE_RUN, H], U8, align_bytes=64, name="first_planes%d" % run
+            )
+            second_planes[run] = keep.tile(
+                [P, TILES_PER_SCALE_RUN, H], U8, align_bytes=64, name="second_planes%d" % run
+            )
         last_plane = keep.tile([P, H], U8, align_bytes=64)
         g_codes = keep.tile([P, FULL_TILES + 1, PAIRS], U32, align_bytes=64)
         g_planes = keep.tile([P, FULL_TILES + 1, PAIRS], U8, align_bytes=64)
@@ -88,11 +99,11 @@ def tile_mpnencoder_pa_k_kernel(tc, f_atoms, f_bonds, adj, W_i_w_words, W_i_w_sc
         nc.vector.memset(adj_row[:], 0.0)
         nc.gpsimd.memset(z_sb[:], 0.0)
 
-        nc.scalar.dma_start(out=adj_row[0:1, :], in_=adj.rearrange("b m n -> (b m n)").unsqueeze(0))
         nc.scalar.dma_start(
             out=x_sb[:],
             in_=f_atoms[:, :, 0 : X_CHUNKS * X_FEATS].rearrange("b m (c j) -> (b m) c j", c=X_CHUNKS),
         )
+        nc.scalar.dma_start(out=adj_row[0:1, :], in_=adj.rearrange("b m n -> (b m n)").unsqueeze(0))
 
         def load_words(words, first_block, blocks, first_part):
             nc.sync.dma_start(
@@ -134,14 +145,14 @@ def tile_mpnencoder_pa_k_kernel(tc, f_atoms, f_bonds, adj, W_i_w_words, W_i_w_sc
         for i in range(FULL_TILES):
             if i == TRANSPOSE_LAST_BEFORE:
                 load_last_tile_features()
-            load_words(first_words[:, i, :], PASS_BLOCKS * i, PASS_BLOCKS, 0)
+            load_words(first_words[i][:], PASS_BLOCKS * i, PASS_BLOCKS, 0)
             if i > 0:
-                load_words(second_words[:, i, :], PASS_BLOCKS * i + COPY_SHIFT, PASS_BLOCKS, 0)
+                load_words(second_words[i][:], PASS_BLOCKS * i + COPY_SHIFT, PASS_BLOCKS, 0)
             if i % TILES_PER_SCALE_RUN == 0:
-                end = i + TILES_PER_SCALE_RUN
-                load_planes(first_planes[:, i:end, :], PASS_BLOCKS * i)
+                run = i // TILES_PER_SCALE_RUN
+                load_planes(first_planes[run][:], PASS_BLOCKS * i)
                 begin = max(i, 1)
-                load_planes(second_planes[:, begin:end, :], PASS_BLOCKS * begin + COPY_SHIFT)
+                load_planes(second_planes[run][:, begin - i :, :], PASS_BLOCKS * begin + COPY_SHIFT)
 
         nc.vector.memset(last_plane[:].bitcast(I32), 0)
         for position, first_block, blocks in (bond_run, rest_first_run, low_second_run, rest_second_run):
@@ -239,9 +250,12 @@ def tile_mpnencoder_pa_k_kernel(tc, f_atoms, f_bonds, adj, W_i_w_words, W_i_w_sc
                 in_=grouped[:].rearrange("p w t -> p (w t)"),
             )
 
-        partners = [[(first_words[:, i, :], first_planes[:, i, :])] for i in range(FULL_TILES)]
-        for i in range(1, FULL_TILES):
-            partners[i].append((second_words[:, i, :], second_planes[:, i, :]))
+        partners = []
+        for i in range(FULL_TILES):
+            run, slot = divmod(i, TILES_PER_SCALE_RUN)
+            partners.append([(first_words[i][:], first_planes[run][:, slot, :])])
+            if i > 0:
+                partners[i].append((second_words[i][:], second_planes[run][:, slot, :]))
         partners.append([(last_words[:], last_plane[:])])
 
         banks = {}

@@ -33,20 +33,25 @@ REST_FEATS = ATOM_FEATS - FULL_TILES * K_PASS
 COPY_SHIFT = (ATOM_FEATS - ONCE_FEATS) // BLOCK
 
 PAIR_TILES = PAIRS // P
-SOURCES_PER_TILE = P // ATOMS
+PARTNERS = ATOMS // PAIR_TILES
 N_COLS = 512
 COL_TILES = H // N_COLS
 
 X_CHUNKS = P // SOURCES
-X_FEATS = FULL_TILES * K_PASS // X_CHUNKS
-X_TILES = X_FEATS // K_PASS
+X_TILES = FULL_TILES // X_CHUNKS
 
-TILES_PER_SCALE_RUN = 4
+TILE_ORDER = tuple(range(FULL_TILES + 1))
+PLANE_RUNS = ((0, 4), (4, 4))
 EARLY_PAIR_TILES = PAIR_TILES - 1
-TRANSPOSE_LAST_BEFORE = 2
+Z_BONDS = PAIR_TILES * 2 * BOND_FEATS
+Z_FEATS = Z_BONDS - 2 * BOND_FEATS + K_PASS
 
-def bank_name(r, c):
-    return "bank%d" % (COL_TILES * r + c)
+
+COPY_HIGH_BEFORE = 6
+
+
+def bank_name(v, c):
+    return "bank%d" % (COL_TILES * v + c)
 
 
 FLOPS = 2 * PAIRS * (2 * ATOM_FEATS - ONCE_FEATS + 2 * BOND_FEATS) * H
@@ -56,7 +61,7 @@ def tile_mpnencoder_pa_k_kernel(tc, f_atoms, f_bonds, adj, W_i_w_words, W_i_w_sc
     nc = tc.nc
     word_rows = W_i_w_words.rearrange("g p n -> (g p) n")
     scale_rows = W_i_w_scales.rearrange("g q n -> (g q) n")
-    out_rows = out.rearrange("b m n h -> (b m n) h")
+    out_rows = out.rearrange("b m n h -> (b m n) h").rearrange("(j v) h -> v j h", v=PAIR_TILES)
 
     with ExitStack() as ctx:
         ctx.enter_context(tc.manual_schedule())
@@ -72,15 +77,16 @@ def tile_mpnencoder_pa_k_kernel(tc, f_atoms, f_bonds, adj, W_i_w_words, W_i_w_sc
             if i > 0:
                 second_words[i] = keep.tile([P, 2 * H], U8, align_bytes=64, name="second_words%d" % i)
         last_words = keep.tile([P, 2 * H], U8, align_bytes=64)
-        first_planes = {}
-        second_planes = {}
-        for run in range(FULL_TILES // TILES_PER_SCALE_RUN):
-            first_planes[run] = keep.tile(
-                [P, TILES_PER_SCALE_RUN, H], U8, align_bytes=64, name="first_planes%d" % run
-            )
-            second_planes[run] = keep.tile(
-                [P, TILES_PER_SCALE_RUN, H], U8, align_bytes=64, name="second_planes%d" % run
-            )
+        first_runs = {}
+        second_runs = {}
+        first_plane = {}
+        second_plane = {}
+        for begin, count in PLANE_RUNS:
+            first_runs[begin] = keep.tile([P, count, H], U8, align_bytes=64, name="first_planes%d" % begin)
+            second_runs[begin] = keep.tile([P, count, H], U8, align_bytes=64, name="second_planes%d" % begin)
+            for k in range(count):
+                first_plane[begin + k] = first_runs[begin][:, k, :]
+                second_plane[begin + k] = second_runs[begin][:, k, :]
         last_plane = keep.tile([P, H], U8, align_bytes=64)
         g_codes = keep.tile([P, FULL_TILES + 1, PAIRS], U32, align_bytes=64)
         g_planes = keep.tile([P, FULL_TILES + 1, PAIRS], U8, align_bytes=64)
@@ -88,22 +94,35 @@ def tile_mpnencoder_pa_k_kernel(tc, f_atoms, f_bonds, adj, W_i_w_words, W_i_w_sc
         identity = keep.tile([P, P], F32)
         ones = keep.tile([P, P], BF16)
         adj_row = keep.tile([P, PAIRS], BF16)
-        adj_x4 = keep.tile([P, PAIRS, PACK], BF16)
-        x_sb = keep.tile([P, X_FEATS], BF16)
-        atoms_t = keep.tile([P, FULL_TILES + 1, SOURCES, PACK], BF16)
+        adj_x4 = {}
+        for v in range(PAIR_TILES):
+            adj_x4[v] = keep.tile([P, P, PACK], BF16, name="adj_x4_%d" % v)
+        x_sb = keep.tile([P, X_TILES * K_PASS], BF16)
+        atoms_t = keep.tile([P, FULL_TILES, SOURCES, PACK], BF16)
+        atoms_last = keep.tile([P, SOURCES, PACK], BF16)
         bonds_t = keep.tile([2 * BLOCK_PARTS, PAIRS, PACK], BF16)
-        z_sb = keep.tile([P, PAIR_TILES, K_PASS], BF16)
+        z_raw = keep.tile([P, PAIR_TILES * BOND_FEATS], BF16)
+        z_sb = keep.tile([P, Z_FEATS], BF16)
 
+        nc.gpsimd.memset(adj_row[:].bitcast(F32), 0.0)
+        nc.gpsimd.memset(z_sb[:, Z_BONDS:Z_FEATS].bitcast(F32), 0.0)
         nc.gpsimd.memset(ones[:], 1.0)
         make_identity(nc, identity[:])
-        nc.vector.memset(adj_row[:], 0.0)
-        nc.gpsimd.memset(z_sb[:], 0.0)
+        nc.gpsimd.memset(atoms_last[:], 0.0)
+        nc.gpsimd.memset(second_runs[4][:].bitcast(F32), 0.0)
+        nc.gpsimd.memset(last_plane[:].bitcast(F32), 0.0)
 
-        nc.scalar.dma_start(
-            out=x_sb[:],
-            in_=f_atoms[:, :, 0 : X_CHUNKS * X_FEATS].rearrange("b m (c j) -> (b m) c j", c=X_CHUNKS),
-        )
         nc.scalar.dma_start(out=adj_row[0:1, :], in_=adj.rearrange("b m n -> (b m n)").unsqueeze(0))
+        nc.scalar.dma_start(
+            out=z_raw[:],
+            in_=f_bonds.rearrange("b m n f -> (b m n) f").rearrange("(j v) f -> j (v f)", v=PAIR_TILES),
+        )
+
+        first_l = TILE_ORDER[0] % X_TILES
+        nc.sync.dma_start(
+            out=x_sb[:],
+            in_=f_atoms[:, :, 0 : FULL_TILES * K_PASS].rearrange("b m (c j) -> (b m) c j", c=X_CHUNKS),
+        )
 
         def load_words(words, first_block, blocks, first_part):
             nc.sync.dma_start(
@@ -111,203 +130,235 @@ def tile_mpnencoder_pa_k_kernel(tc, f_atoms, f_bonds, adj, W_i_w_words, W_i_w_sc
                 in_=word_rows[BLOCK_PARTS * first_block : BLOCK_PARTS * (first_block + blocks), :].bitcast(I32),
             )
 
+        def load_tile_words(i):
+            load_words(first_words[i][:], PASS_BLOCKS * i, PASS_BLOCKS, 0)
+            if i > 0:
+                load_words(second_words[i][:], PASS_BLOCKS * i + COPY_SHIFT, PASS_BLOCKS, 0)
+
         def load_planes(planes, first_block):
             count = planes.shape[1]
-            nc.vector.memset(planes.bitcast(I32), 0)
             rows = scale_rows[first_block : first_block + PASS_BLOCKS * count, :].rearrange(
                 "(i q s) n -> s q i n", q=4, s=4
             )
             for s in range(4):
                 nc.sync.dma_start(out=planes[s:P:32, :, :].bitcast(I32), in_=rows[s].bitcast(I32))
 
-        rest_blocks = REST_FEATS // BLOCK
-        once_blocks = ONCE_FEATS // BLOCK
-        atom_blocks = ATOM_FEATS // BLOCK
-        bond_run = (0, atom_blocks + COPY_SHIFT, 2)
-        rest_first_run = (2, FULL_TILES * PASS_BLOCKS, rest_blocks)
-        low_second_run = (2 + rest_blocks, atom_blocks, PASS_BLOCKS - once_blocks)
-        rest_second_run = (PASS_BLOCKS - rest_blocks, FULL_TILES * PASS_BLOCKS + COPY_SHIFT, rest_blocks)
+        def load_last_tile():
+            rest_blocks = REST_FEATS // BLOCK
+            once_blocks = ONCE_FEATS // BLOCK
+            atom_blocks = ATOM_FEATS // BLOCK
+            bond_run = (0, atom_blocks + COPY_SHIFT, 2)
+            rest_first_run = (2, FULL_TILES * PASS_BLOCKS, rest_blocks)
+            rest_second_run = (2 + rest_blocks, FULL_TILES * PASS_BLOCKS + COPY_SHIFT, rest_blocks)
+            low_second_run = (once_blocks, atom_blocks, PASS_BLOCKS - once_blocks)
+            for position, first_block, blocks in (bond_run, rest_first_run, rest_second_run, low_second_run):
+                load_words(last_words[:], first_block, blocks, BLOCK_PARTS * position)
+                done = 0
+                while done < blocks:
+                    q = position + done
+                    step = min(4 - q % 4, blocks - done)
+                    part = 32 * (q // 4) + q % 4
+                    nc.sync.dma_start(
+                        out=last_plane[part : part + step, :].bitcast(I32),
+                        in_=scale_rows[first_block + done : first_block + done + step, :].bitcast(I32),
+                    )
+                    done += step
 
-        def load_last_tile_features():
-            bond_rows = f_bonds.rearrange("b m n f -> (b m n) f").rearrange("(s j) f -> j s f", j=P)
-            for position in range(bond_run[0], bond_run[0] + bond_run[2]):
-                nc.sync.dma_start(out=z_sb[:, :, BLOCK * position : BLOCK * (position + 1)], in_=bond_rows)
-            for position, first_feat, blocks in (
-                (rest_first_run[0], FULL_TILES * K_PASS, rest_blocks),
-                (low_second_run[0], ONCE_FEATS, PASS_BLOCKS - once_blocks),
-                (rest_second_run[0], FULL_TILES * K_PASS, rest_blocks),
-            ):
-                nc.sync.dma_start(
-                    out=z_sb[0:SOURCES, 0, BLOCK * position : BLOCK * (position + blocks)],
-                    in_=f_atoms[:, :, first_feat : first_feat + BLOCK * blocks].rearrange("b m j -> (b m) j"),
-                )
+        load_tile_words(0)
+        nc.vector.memset(first_runs[0][:].bitcast(I32), 0)
+        load_planes(first_runs[0][:], 0)
+        load_tile_words(1)
+        nc.vector.memset(second_runs[0][:, 1:, :].bitcast(I32), 0)
+        load_planes(second_runs[0][:, 1:, :], PASS_BLOCKS + COPY_SHIFT)
+        load_tile_words(2)
+        load_tile_words(3)
+        nc.vector.memset(first_runs[4][:].bitcast(I32), 0)
+        load_planes(first_runs[4][:], PASS_BLOCKS * 4)
+        load_tile_words(4)
+        load_planes(second_runs[4][:], PASS_BLOCKS * 4 + COPY_SHIFT)
+        load_tile_words(5)
 
-        for i in range(FULL_TILES):
-            if i == TRANSPOSE_LAST_BEFORE:
-                load_last_tile_features()
-            load_words(first_words[i][:], PASS_BLOCKS * i, PASS_BLOCKS, 0)
-            if i > 0:
-                load_words(second_words[i][:], PASS_BLOCKS * i + COPY_SHIFT, PASS_BLOCKS, 0)
-            if i % TILES_PER_SCALE_RUN == 0:
-                run = i // TILES_PER_SCALE_RUN
-                load_planes(first_planes[run][:], PASS_BLOCKS * i)
-                begin = max(i, 1)
-                load_planes(second_planes[run][:, begin - i :, :], PASS_BLOCKS * begin + COPY_SHIFT)
+        def late_loads():
+            rest_parts = REST_FEATS // PACK
+            rest_view = f_atoms[:, :, FULL_TILES * K_PASS : ATOM_FEATS].rearrange("b m (p t) -> p (b m) t", t=PACK)
+            for copy in range(2):
+                first = 2 * BLOCK_PARTS + rest_parts * copy
+                nc.sync.dma_start(out=atoms_last[first : first + rest_parts, :, :], in_=rest_view)
+            load_tile_words(6)
+            load_tile_words(7)
+            load_last_tile()
 
-        nc.vector.memset(last_plane[:].bitcast(I32), 0)
-        for position, first_block, blocks in (bond_run, rest_first_run, low_second_run, rest_second_run):
-            load_words(last_words[:], first_block, blocks, BLOCK_PARTS * position)
-            done = 0
-            while done < blocks:
-                q = position + done
-                step = min(4 - q % 4, blocks - done)
-                part = 32 * (q // 4) + q % 4
-                nc.sync.dma_start(
-                    out=last_plane[part : part + step, :].bitcast(I32),
-                    in_=scale_rows[first_block + done : first_block + done + step, :].bitcast(I32),
-                )
-                done += step
+        nc.scalar.copy(
+            out=z_sb[:, 0:Z_BONDS].rearrange("j (v c f) -> j v c f", c=2, f=BOND_FEATS),
+            in_=z_raw[:]
+            .rearrange("j (v f) -> j v f", f=BOND_FEATS)
+            .unsqueeze(2)
+            .to_broadcast([P, PAIR_TILES, 2, BOND_FEATS]),
+        )
 
-        adj_ps = psum.tile([P, PAIRS], F32, tag=bank_name(EARLY_PAIR_TILES, 0))
-        xt = psum.tile([P, X_TILES, 2, P], F32, tag=bank_name(EARLY_PAIR_TILES, 1))
-        nc.tensor.matmul(out=adj_ps[:], lhsT=ones[:], rhs=adj_row[:], start=True, stop=True)
-        x_words = x_sb[:].bitcast(F32)
-        words_per_tile = K_PASS // 2
-        for l in range(X_TILES):
+        head_ps = psum.tile([P, 3, P], F32, tag=bank_name(2, 0))
+        adj_ps = psum.tile([P, PAIRS], F32, tag=bank_name(2, 1))
+        other_ps = psum.tile([P, 2, P], F32, tag=bank_name(1, 1))
+        xt = {first_l: head_ps, 1 - first_l: other_ps}
+
+        def transpose_atoms(l):
+            x_words = x_sb[:, K_PASS * l : K_PASS * (l + 1)].bitcast(F32)
             for u in range(2):
-                nc.tensor.transpose(
-                    xt[:, l, u, :],
-                    x_words[:, words_per_tile * l + u : words_per_tile * (l + 1) : 2],
-                    identity[:],
-                )
-        atoms_words = atoms_t[:].bitcast(F32)
+                nc.tensor.transpose(xt[l][:, u, :], x_words[:, u : K_PASS // 2 : 2], identity[:])
 
-        def atoms_out_of_psum(copy, l):
-            copy(
-                out=atoms_words[:, l:FULL_TILES:X_TILES, :, :],
-                in_=xt[:, l, :, :].rearrange("p u (a c) -> p c a u", c=X_CHUNKS),
+        transpose_atoms(first_l)
+        nc.tensor.matmul(
+            out=head_ps[:, 2, :], lhsT=ones[:], rhs=adj_row[:, 0:PAIRS:PAIR_TILES], start=True, stop=True
+        )
+        nc.tensor.matmul(out=adj_ps[:], lhsT=ones[:], rhs=adj_row[:], start=True, stop=True)
+        transpose_atoms(1 - first_l)
+        z_words = z_sb[:].bitcast(F32)
+        slabs_per_bank = N_COLS // (2 * P)
+        zt = {}
+        for half in range(PAIR_TILES // slabs_per_bank):
+            zt[half] = psum.tile(
+                [P, slabs_per_bank, 2, P], F32, name="zt%d" % half, tag=bank_name(EARLY_PAIR_TILES, half)
             )
-
-        atoms_out_of_psum(nc.vector.tensor_copy, 0)
-        for r in range(PAIR_TILES):
-            pairs = slice(P * r, P * (r + 1))
-            nc.scalar.copy(
-                out=adj_x4[:, pairs, :],
-                in_=adj_ps[:, pairs].unsqueeze(2).to_broadcast([P, P, PACK]),
-            )
-        atoms_out_of_psum(nc.scalar.copy, 1)
-
-        def transpose_last_tile():
-            z_words = z_sb[:].bitcast(F32)
-            bonds_words = bonds_t[:].bitcast(F32)
-            bond_parts = slice(0, 2 * BLOCK_PARTS)
-            slabs_per_bank = N_COLS // (2 * P)
-            for half in range(PAIR_TILES // slabs_per_bank):
-                zt = psum.tile([P, slabs_per_bank, 2, P], F32, name="zt", tag=bank_name(EARLY_PAIR_TILES, half))
-                for s in range(slabs_per_bank):
-                    for u in range(2):
-                        nc.tensor.transpose(
-                            zt[:, s, u, :], z_words[:, slabs_per_bank * half + s, u : K_PASS // 2 : 2], identity[:]
-                        )
-                nc.scalar.copy(
-                    out=bonds_words[:, slabs_per_bank * P * half : slabs_per_bank * P * (half + 1), :].rearrange(
-                        "p (s j) u -> p s j u", j=P
-                    ),
-                    in_=zt[bond_parts, :, :, :].rearrange("p s u j -> p s j u"),
-                )
-                if half == 0:
-                    nc.scalar.copy(
-                        out=atoms_words[:, LAST, :, :],
-                        in_=zt[:, 0, :, 0:SOURCES].rearrange("p u a -> p a u"),
+            for s in range(slabs_per_bank):
+                first = BOND_FEATS * (slabs_per_bank * half + s)
+                for u in range(2):
+                    nc.tensor.transpose(
+                        zt[half][:, s, u, :], z_words[:, first + u : first + K_PASS // 2 : 2], identity[:]
                     )
 
-        def gate(i, r):
-            pairs = slice(P * r, P * (r + 1))
+        atoms_words = atoms_t[:].bitcast(F32)
+        bonds_words = bonds_t[:].bitcast(F32)
+
+        def gate(i, v, adj_of_pairs):
             grouped = stage.tile([P, P, PACK], BF16, align_bytes=64, name="grouped")
             nc.vector.tensor_tensor(
-                out=grouped[:].rearrange("p (a n) t -> p a n t", n=ATOMS),
-                in0=atoms_t[:, i, SOURCES_PER_TILE * r : SOURCES_PER_TILE * (r + 1), :]
+                out=grouped[:].rearrange("p (a k) t -> p a k t", k=PARTNERS),
+                in0=(atoms_last[:] if i == LAST else atoms_t[:, i, :, :])
                 .unsqueeze(2)
-                .to_broadcast([P, SOURCES_PER_TILE, ATOMS, PACK]),
-                in1=adj_x4[:, pairs, :].rearrange("p (a n) t -> p a n t", n=ATOMS),
+                .to_broadcast([P, SOURCES, PARTNERS, PACK]),
+                in1=adj_of_pairs,
                 op=MULT,
             )
             if i == LAST:
                 bond_parts = slice(0, 2 * BLOCK_PARTS)
                 nc.vector.tensor_tensor(
                     out=grouped[bond_parts, :, :],
-                    in0=bonds_t[:, pairs, :],
-                    in1=adj_x4[bond_parts, pairs, :],
+                    in0=bonds_t[:, P * v : P * (v + 1), :],
+                    in1=adj_x4[v][bond_parts, :, :],
                     op=MULT,
                 )
             return grouped
 
-        def quantise(i, r, grouped):
-            pairs = slice(P * r, P * (r + 1))
+        def gate_from_sbuf(i, v):
+            return gate(i, v, adj_x4[v][:].rearrange("p (a k) t -> p a k t", k=PARTNERS))
+
+        def quantise(i, v, grouped):
+            pairs = slice(P * v, P * (v + 1))
             nc.vector.quantize_mx(
                 out=g_codes[:, i, pairs].bitcast(FP8X4),
                 scales=g_planes[:, i, pairs],
                 in_=grouped[:].rearrange("p w t -> p (w t)"),
             )
 
+        first_tile = TILE_ORDER[0]
+        first_chunk = first_tile // X_TILES
+        by_chunk = head_ps[:, 0:2, :].rearrange("p u (a c) -> p c a u", c=X_CHUNKS)
+        nc.vector.tensor_copy(out=atoms_words[:, first_tile, :, :], in_=by_chunk[:, first_chunk, :, :])
+        gated = gate(
+            first_tile,
+            0,
+            head_ps[:, 2, :]
+            .rearrange("p (a k) -> p a k", k=PARTNERS)
+            .unsqueeze(3)
+            .to_broadcast([P, SOURCES, PARTNERS, PACK]),
+        )
+        nc.vector.tensor_copy(
+            out=atoms_words[:, first_tile + X_TILES : FULL_TILES : X_TILES, :, :],
+            in_=by_chunk[:, first_chunk + 1 : X_CHUNKS, :, :],
+        )
+
+        def spread_adj(v):
+            nc.scalar.copy(
+                out=adj_x4[v][:],
+                in_=adj_ps[:, v:PAIRS:PAIR_TILES].unsqueeze(2).to_broadcast([P, P, PACK]),
+            )
+
+        spread_adj(1)
+        spread_adj(2)
+        spread_adj(0)
+        nc.scalar.copy(
+            out=atoms_words[:, 1 - first_l : FULL_TILES : X_TILES, :, :],
+            in_=other_ps[:].rearrange("p u (a c) -> p c a u", c=X_CHUNKS),
+        )
+        spread_adj(3)
+        bond_parts = slice(0, 2 * BLOCK_PARTS)
+        for half in range(PAIR_TILES // slabs_per_bank):
+            nc.scalar.copy(
+                out=bonds_words[:, slabs_per_bank * P * half : slabs_per_bank * P * (half + 1), :].rearrange(
+                    "p (s j) u -> p s j u", j=P
+                ),
+                in_=zt[half][bond_parts, :, :, :].rearrange("p s u j -> p s j u"),
+            )
+
         partners = []
         for i in range(FULL_TILES):
-            run, slot = divmod(i, TILES_PER_SCALE_RUN)
-            partners.append([(first_words[i][:], first_planes[run][:, slot, :])])
+            partners.append([(first_words[i][:], first_plane[i])])
             if i > 0:
-                partners[i].append((second_words[i][:], second_planes[run][:, slot, :]))
+                partners[i].append((second_words[i][:], second_plane[i]))
         partners.append([(last_words[:], last_plane[:])])
 
         banks = {}
 
-        def open_banks(r):
+        def open_banks(v):
             for c in range(COL_TILES):
-                banks[(r, c)] = psum.tile([P, N_COLS], F32, name=bank_name(r, c), tag=bank_name(r, c))
+                banks[(v, c)] = psum.tile([P, N_COLS], F32, name=bank_name(v, c), tag=bank_name(v, c))
 
-        def mx_passes(i, r, c):
-            pairs = slice(P * r, P * (r + 1))
-            for words, plane in partners[i]:
+        def mx_passes(i, v, c):
+            pairs = slice(P * v, P * (v + 1))
+            for number, (words, plane) in enumerate(partners[i]):
                 nc.tensor.matmul_mx(
-                    out=banks[(r, c)][:],
+                    out=banks[(v, c)][:],
                     lhsT=g_codes[:, i, pairs].bitcast(FP8X4),
                     lhsT_scale=g_planes[:, i, pairs],
                     rhs=words[:, 2 * N_COLS * c : 2 * N_COLS * (c + 1)].bitcast(FP4X4),
                     rhs_scale=plane[:, N_COLS * c : N_COLS * (c + 1)],
-                    start=(i == 0),
-                    stop=(i == LAST),
+                    start=(i == TILE_ORDER[0] and number == 0),
+                    stop=(i == TILE_ORDER[-1]),
                 )
 
-        def store_bank(r, c):
+        def store_bank(v, c):
             result = results.tile([P, N_COLS], F32, name="result")
             if c % 2 == 0:
-                nc.scalar.copy(out=result[:], in_=banks[(r, c)][:])
+                nc.scalar.copy(out=result[:], in_=banks[(v, c)][:])
             else:
-                nc.vector.tensor_copy(out=result[:], in_=banks[(r, c)][:])
-            nc.sync.dma_start(out=out_rows[P * r : P * (r + 1), N_COLS * c : N_COLS * (c + 1)], in_=result[:])
+                nc.vector.tensor_copy(out=result[:], in_=banks[(v, c)][:])
+            nc.sync.dma_start(out=out_rows[v][:, N_COLS * c : N_COLS * (c + 1)], in_=result[:])
 
-        for r in range(EARLY_PAIR_TILES):
-            open_banks(r)
-        tiles = range(FULL_TILES + 1)
-        steps = [(i, r) for i in tiles for r in range(EARLY_PAIR_TILES)]
-        steps.extend([(i, r) for r in range(EARLY_PAIR_TILES, PAIR_TILES) for i in tiles])
-        gated = gate(*steps[0])
-        for index, (i, r) in enumerate(steps):
-            if (i, r) == (TRANSPOSE_LAST_BEFORE, 0):
-                transpose_last_tile()
+        for v in range(EARLY_PAIR_TILES):
+            open_banks(v)
+        steps = [(i, v) for i in TILE_ORDER for v in range(EARLY_PAIR_TILES)]
+        steps.extend([(i, v) for v in range(EARLY_PAIR_TILES, PAIR_TILES) for i in TILE_ORDER])
+        for index, (i, v) in enumerate(steps):
+            if index == COPY_HIGH_BEFORE:
+                high = slice(P // 2, P)
+                nc.vector.tensor_copy(out=atoms_last[high, :, :], in_=atoms_t[high, 0, :, :])
+                late_loads()
             ready = gated
-            if index + 1 < len(steps):
-                gated = gate(*steps[index + 1])
-            quantise(i, r, ready)
-            if r < EARLY_PAIR_TILES:
+            if 0 < index < len(steps) - 1:
+                gated = gate_from_sbuf(*steps[index + 1])
+            quantise(i, v, ready)
+            if index == 0:
+                gated = gate_from_sbuf(*steps[1])
+            if v < EARLY_PAIR_TILES:
                 for c in range(COL_TILES):
-                    mx_passes(i, r, c)
+                    mx_passes(i, v, c)
 
-        for r in range(EARLY_PAIR_TILES):
+        for v in range(EARLY_PAIR_TILES):
             for c in range(COL_TILES):
-                store_bank(r, c)
-        for r in range(EARLY_PAIR_TILES, PAIR_TILES):
-            open_banks(r)
+                store_bank(v, c)
+        for v in range(EARLY_PAIR_TILES, PAIR_TILES):
+            open_banks(v)
             for c in range(COL_TILES):
-                for i in tiles:
-                    mx_passes(i, r, c)
-                store_bank(r, c)
+                for i in TILE_ORDER:
+                    mx_passes(i, v, c)
+                store_bank(v, c)

@@ -50,6 +50,9 @@ Z_FEATS = Z_BONDS - 2 * BOND_FEATS + K_PASS
 COPY_HIGH_BEFORE = 6
 
 
+WARM_MATMULS = 4
+
+
 def bank_name(v, c):
     return "bank%d" % (COL_TILES * v + c)
 
@@ -92,6 +95,7 @@ def tile_mpnencoder_pa_k_kernel(tc, f_atoms, f_bonds, adj, W_i_w_words, W_i_w_sc
         g_planes = keep.tile([P, FULL_TILES + 1, PAIRS], U8, align_bytes=64)
 
         identity = keep.tile([P, P], F32)
+        warm = keep.tile([P, N_COLS], BF16)
         ones = keep.tile([P, P], BF16)
         adj_row = keep.tile([P, PAIRS], BF16)
         adj_x4 = {}
@@ -103,6 +107,11 @@ def tile_mpnencoder_pa_k_kernel(tc, f_atoms, f_bonds, adj, W_i_w_words, W_i_w_sc
         bonds_t = keep.tile([2 * BLOCK_PARTS, PAIRS, PACK], BF16)
         z_raw = keep.tile([P, PAIR_TILES * BOND_FEATS], BF16)
         z_sb = keep.tile([P, Z_FEATS], BF16)
+
+        nc.vector.memset(warm[:].bitcast(I32), 0)
+        warm_ps = psum.tile([P, N_COLS], F32, tag=bank_name(0, 0))
+        for number in range(WARM_MATMULS):
+            nc.tensor.matmul(out=warm_ps[:], lhsT=warm[:, 0:P], rhs=warm[:], start=True, stop=True)
 
         nc.gpsimd.memset(adj_row[:].bitcast(F32), 0.0)
         nc.gpsimd.memset(z_sb[:, Z_BONDS:Z_FEATS].bitcast(F32), 0.0)

@@ -40,8 +40,7 @@ COL_TILES = H // N_COLS
 X_CHUNKS = P // SOURCES
 X_TILES = FULL_TILES // X_CHUNKS
 
-TILE_ORDER = tuple(range(FULL_TILES + 1))
-PLANE_RUNS = ((0, 4), (4, 4))
+TILE_ORDER = tuple(range(1, FULL_TILES)) + (0, LAST)
 EARLY_PAIR_TILES = PAIR_TILES - 1
 Z_BONDS = PAIR_TILES * 2 * BOND_FEATS
 Z_FEATS = Z_BONDS - 2 * BOND_FEATS + K_PASS
@@ -73,23 +72,15 @@ def tile_mpnencoder_pa_k_kernel(tc, f_atoms, f_bonds, adj, W_i_w_words, W_i_w_sc
         results = ctx.enter_context(tc.tile_pool(name="results", bufs=4))
         psum = ctx.enter_context(tc.psum_pool(name="psum", bufs=1))
 
-        first_words = {}
-        second_words = {}
-        for i in range(FULL_TILES):
-            first_words[i] = keep.tile([P, 2 * H], U8, align_bytes=64, name="first_words%d" % i)
-            if i > 0:
-                second_words[i] = keep.tile([P, 2 * H], U8, align_bytes=64, name="second_words%d" % i)
+        both_words = {}
+        for i in range(1, FULL_TILES):
+            both_words[i] = keep.tile([P, 2, 2 * H], U8, align_bytes=64, name="both_words%d" % i)
+        zero_words = keep.tile([P, 2 * H], U8, align_bytes=64)
         last_words = keep.tile([P, 2 * H], U8, align_bytes=64)
-        first_runs = {}
-        second_runs = {}
-        first_plane = {}
-        second_plane = {}
-        for begin, count in PLANE_RUNS:
-            first_runs[begin] = keep.tile([P, count, H], U8, align_bytes=64, name="first_planes%d" % begin)
-            second_runs[begin] = keep.tile([P, count, H], U8, align_bytes=64, name="second_planes%d" % begin)
-            for k in range(count):
-                first_plane[begin + k] = first_runs[begin][:, k, :]
-                second_plane[begin + k] = second_runs[begin][:, k, :]
+        opening = TILE_ORDER[0]
+        opening_planes = keep.tile([P, 2, H], U8, align_bytes=64)
+        first_planes = keep.tile([P, FULL_TILES, H], U8, align_bytes=64)
+        second_planes = keep.tile([P, FULL_TILES - 2, H], U8, align_bytes=64)
         last_plane = keep.tile([P, H], U8, align_bytes=64)
         g_codes = keep.tile([P, FULL_TILES + 1, PAIRS], U32, align_bytes=64)
         g_planes = keep.tile([P, FULL_TILES + 1, PAIRS], U8, align_bytes=64)
@@ -118,7 +109,7 @@ def tile_mpnencoder_pa_k_kernel(tc, f_atoms, f_bonds, adj, W_i_w_words, W_i_w_sc
         nc.gpsimd.memset(ones[:], 1.0)
         make_identity(nc, identity[:])
         nc.gpsimd.memset(atoms_last[:], 0.0)
-        nc.gpsimd.memset(second_runs[4][:].bitcast(F32), 0.0)
+        nc.gpsimd.memset(second_planes[:].bitcast(F32), 0.0)
         nc.gpsimd.memset(last_plane[:].bitcast(F32), 0.0)
 
         nc.scalar.dma_start(out=adj_row[0:1, :], in_=adj.rearrange("b m n -> (b m n)").unsqueeze(0))
@@ -139,10 +130,27 @@ def tile_mpnencoder_pa_k_kernel(tc, f_atoms, f_bonds, adj, W_i_w_words, W_i_w_sc
                 in_=word_rows[BLOCK_PARTS * first_block : BLOCK_PARTS * (first_block + blocks), :].bitcast(I32),
             )
 
+        def both_copies(rows, per_block):
+            length = COPY_SHIFT * per_block
+            begin = rows.shape[0] - 2 * length
+            return rows[begin:, :].rearrange("(e x) n -> e x n", e=2), begin // per_block
+
         def load_tile_words(i):
-            load_words(first_words[i][:], PASS_BLOCKS * i, PASS_BLOCKS, 0)
-            if i > 0:
-                load_words(second_words[i][:], PASS_BLOCKS * i + COPY_SHIFT, PASS_BLOCKS, 0)
+            if i == 0:
+                load_words(zero_words[:], 0, PASS_BLOCKS, 0)
+                return
+            view, block0 = both_copies(word_rows.bitcast(I32), BLOCK_PARTS)
+            first = BLOCK_PARTS * (PASS_BLOCKS * i - block0)
+            nc.sync.dma_start(
+                out=both_words[i][:].bitcast(I32), in_=view[:, first : first + P, :].rearrange("e p n -> p e n")
+            )
+
+        def load_opening_planes():
+            view, block0 = both_copies(scale_rows.bitcast(I32), 1)
+            first = PASS_BLOCKS * opening - block0
+            rows = view[:, first : first + PASS_BLOCKS, :].rearrange("e (q s) n -> s q e n", s=4)
+            for s in range(4):
+                nc.sync.dma_start(out=opening_planes[s:P:32, :, :].bitcast(I32), in_=rows[s])
 
         def load_planes(planes, first_block):
             count = planes.shape[1]
@@ -173,18 +181,15 @@ def tile_mpnencoder_pa_k_kernel(tc, f_atoms, f_bonds, adj, W_i_w_words, W_i_w_sc
                     )
                     done += step
 
-        load_tile_words(0)
-        nc.vector.memset(first_runs[0][:].bitcast(I32), 0)
-        load_planes(first_runs[0][:], 0)
-        load_tile_words(1)
-        nc.vector.memset(second_runs[0][:, 1:, :].bitcast(I32), 0)
-        load_planes(second_runs[0][:, 1:, :], PASS_BLOCKS + COPY_SHIFT)
+        load_tile_words(opening)
+        nc.vector.memset(opening_planes[:].bitcast(I32), 0)
+        load_opening_planes()
         load_tile_words(2)
+        nc.vector.memset(first_planes[:].bitcast(I32), 0)
+        load_planes(first_planes[:], 0)
+        load_planes(second_planes[:], PASS_BLOCKS * 2 + COPY_SHIFT)
         load_tile_words(3)
-        nc.vector.memset(first_runs[4][:].bitcast(I32), 0)
-        load_planes(first_runs[4][:], PASS_BLOCKS * 4)
         load_tile_words(4)
-        load_planes(second_runs[4][:], PASS_BLOCKS * 4 + COPY_SHIFT)
         load_tile_words(5)
 
         def late_loads():
@@ -195,6 +200,7 @@ def tile_mpnencoder_pa_k_kernel(tc, f_atoms, f_bonds, adj, W_i_w_words, W_i_w_sc
                 nc.sync.dma_start(out=atoms_last[first : first + rest_parts, :, :], in_=rest_view)
             load_tile_words(6)
             load_tile_words(7)
+            load_tile_words(0)
             load_last_tile()
 
         nc.scalar.copy(
@@ -310,10 +316,13 @@ def tile_mpnencoder_pa_k_kernel(tc, f_atoms, f_bonds, adj, W_i_w_words, W_i_w_sc
             )
 
         partners = []
-        for i in range(FULL_TILES):
-            partners.append([(first_words[i][:], first_plane[i])])
-            if i > 0:
-                partners[i].append((second_words[i][:], second_plane[i]))
+        partners.append([(zero_words[:], first_planes[:, 0, :])])
+        for i in range(1, FULL_TILES):
+            if i == opening:
+                planes = (opening_planes[:, 0, :], opening_planes[:, 1, :])
+            else:
+                planes = (first_planes[:, i, :], second_planes[:, i - 2, :])
+            partners.append([(both_words[i][:, 0, :], planes[0]), (both_words[i][:, 1, :], planes[1])])
         partners.append([(last_words[:], last_plane[:])])
 
         banks = {}

@@ -52,6 +52,9 @@ COPY_HIGH_BEFORE = 6
 WARM_MATMULS = 4
 
 
+PLANE_RUNS = ((2, 2), (4, 4))
+
+
 def bank_name(v, c):
     return "bank%d" % (COL_TILES * v + c)
 
@@ -79,8 +82,15 @@ def tile_mpnencoder_pa_k_kernel(tc, f_atoms, f_bonds, adj, W_i_w_words, W_i_w_sc
         last_words = keep.tile([P, 2 * H], U8, align_bytes=64)
         opening = TILE_ORDER[0]
         opening_planes = keep.tile([P, 2, H], U8, align_bytes=64)
-        first_planes = keep.tile([P, FULL_TILES, H], U8, align_bytes=64)
-        second_planes = keep.tile([P, FULL_TILES - 2, H], U8, align_bytes=64)
+        first_runs = {}
+        second_runs = {}
+        run_of = {}
+        for begin, count in PLANE_RUNS:
+            first_runs[begin] = keep.tile([P, count, H], U8, align_bytes=64, name="first_planes%d" % begin)
+            second_runs[begin] = keep.tile([P, count, H], U8, align_bytes=64, name="second_planes%d" % begin)
+            for k in range(count):
+                run_of[begin + k] = begin
+        zero_plane = keep.tile([P, 1, H], U8, align_bytes=64)
         last_plane = keep.tile([P, H], U8, align_bytes=64)
         g_codes = keep.tile([P, FULL_TILES + 1, PAIRS], U32, align_bytes=64)
         g_planes = keep.tile([P, FULL_TILES + 1, PAIRS], U8, align_bytes=64)
@@ -109,7 +119,8 @@ def tile_mpnencoder_pa_k_kernel(tc, f_atoms, f_bonds, adj, W_i_w_words, W_i_w_sc
         nc.gpsimd.memset(ones[:], 1.0)
         make_identity(nc, identity[:])
         nc.gpsimd.memset(atoms_last[:], 0.0)
-        nc.gpsimd.memset(second_planes[:].bitcast(F32), 0.0)
+        nc.gpsimd.memset(second_runs[4][:].bitcast(F32), 0.0)
+        nc.gpsimd.memset(zero_plane[:].bitcast(F32), 0.0)
         nc.gpsimd.memset(last_plane[:].bitcast(F32), 0.0)
 
         nc.scalar.dma_start(out=adj_row[0:1, :], in_=adj.rearrange("b m n -> (b m n)").unsqueeze(0))
@@ -185,11 +196,15 @@ def tile_mpnencoder_pa_k_kernel(tc, f_atoms, f_bonds, adj, W_i_w_words, W_i_w_sc
         nc.vector.memset(opening_planes[:].bitcast(I32), 0)
         load_opening_planes()
         load_tile_words(2)
-        nc.vector.memset(first_planes[:].bitcast(I32), 0)
-        load_planes(first_planes[:], 0)
-        load_planes(second_planes[:], PASS_BLOCKS * 2 + COPY_SHIFT)
+        nc.vector.memset(first_runs[2][:].bitcast(I32), 0)
+        load_planes(first_runs[2][:], PASS_BLOCKS * 2)
+        nc.vector.memset(second_runs[2][:].bitcast(I32), 0)
+        load_planes(second_runs[2][:], PASS_BLOCKS * 2 + COPY_SHIFT)
         load_tile_words(3)
         load_tile_words(4)
+        nc.vector.memset(first_runs[4][:].bitcast(I32), 0)
+        load_planes(first_runs[4][:], PASS_BLOCKS * 4)
+        load_planes(second_runs[4][:], PASS_BLOCKS * 4 + COPY_SHIFT)
         load_tile_words(5)
 
         def late_loads():
@@ -200,6 +215,7 @@ def tile_mpnencoder_pa_k_kernel(tc, f_atoms, f_bonds, adj, W_i_w_words, W_i_w_sc
                 nc.sync.dma_start(out=atoms_last[first : first + rest_parts, :, :], in_=rest_view)
             load_tile_words(6)
             load_tile_words(7)
+            load_planes(zero_plane[:], 0)
             load_tile_words(0)
             load_last_tile()
 
@@ -316,12 +332,13 @@ def tile_mpnencoder_pa_k_kernel(tc, f_atoms, f_bonds, adj, W_i_w_words, W_i_w_sc
             )
 
         partners = []
-        partners.append([(zero_words[:], first_planes[:, 0, :])])
+        partners.append([(zero_words[:], zero_plane[:, 0, :])])
         for i in range(1, FULL_TILES):
             if i == opening:
                 planes = (opening_planes[:, 0, :], opening_planes[:, 1, :])
             else:
-                planes = (first_planes[:, i, :], second_planes[:, i - 2, :])
+                begin = run_of[i]
+                planes = (first_runs[begin][:, i - begin, :], second_runs[begin][:, i - begin, :])
             partners.append([(both_words[i][:, 0, :], planes[0]), (both_words[i][:, 1, :], planes[1])])
         partners.append([(last_words[:], last_plane[:])])
 

@@ -362,6 +362,15 @@ def tile_mpnencoder_pa_k_kernel(tc, f_atoms, f_bonds, adj, W_i_w_words, W_i_w_sc
                 )
 
         def store_bank(v, c):
+            if (v, c) == (PAIR_TILES - 1, COL_TILES - 1):
+                for half, queue in enumerate((nc.sync, nc.scalar)):
+                    cols = slice(N_COLS // 2 * half, N_COLS // 2 * (half + 1))
+                    half_result = results.tile([P, N_COLS // 2], F32, name="half_result")
+                    nc.vector.tensor_copy(out=half_result[:], in_=banks[(v, c)][:, cols])
+                    queue.dma_start(
+                        out=out_rows[v][:, N_COLS * c + cols.start : N_COLS * c + cols.stop], in_=half_result[:]
+                    )
+                return
             result = results.tile([P, N_COLS], F32, name="result")
             if c % 2 == 0:
                 nc.scalar.copy(out=result[:], in_=banks[(v, c)][:])

@@ -123,7 +123,6 @@ def tile_mpnencoder_pa_k_kernel(tc, f_atoms, f_bonds, adj, W_i_w_words, W_i_w_sc
         nc.gpsimd.memset(zero_plane[:].bitcast(F32), 0.0)
         nc.gpsimd.memset(last_plane[:].bitcast(F32), 0.0)
 
-        nc.scalar.dma_start(out=adj_row[0:1, :], in_=adj.rearrange("b m n -> (b m n)").unsqueeze(0))
         nc.scalar.dma_start(
             out=z_raw[:],
             in_=f_bonds.rearrange("b m n f -> (b m n) f").rearrange("(j v) f -> j (v f)", v=PAIR_TILES),
@@ -134,6 +133,7 @@ def tile_mpnencoder_pa_k_kernel(tc, f_atoms, f_bonds, adj, W_i_w_words, W_i_w_sc
             out=x_sb[:],
             in_=f_atoms[:, :, 0 : FULL_TILES * K_PASS].rearrange("b m (c j) -> (b m) c j", c=X_CHUNKS),
         )
+        nc.sync.dma_start(out=adj_row[0:1, :], in_=adj.rearrange("b m n -> (b m n)").unsqueeze(0))
 
         def load_words(words, first_block, blocks, first_part):
             nc.sync.dma_start(

from contextlib import ExitStack

import concourse.mybir as mybir
from concourse.masks import make_identity

BF16 = mybir.dt.bfloat16
F32 = mybir.dt.float32
I32 = mybir.dt.int32
U8 = mybir.dt.uint8
U32 = mybir.dt.uint32
FP8X4 = mybir.dt.float8_e4m3fn_x4
FP4X4 = mybir.dt.float4_e2m1fn_x4
MULT = mybir.AluOpType.mult

P = 128
PACK = 4
K_PASS = P * PACK
BLOCK = 32
BLOCK_PARTS = BLOCK // PACK
PASS_BLOCKS = K_PASS // BLOCK

ATOMS = 16
SOURCES = 32
PAIRS = SOURCES * ATOMS
ATOM_FEATS = 4192
ONCE_FEATS = 256
BOND_FEATS = 32
H = 1024

FULL_TILES = ATOM_FEATS // K_PASS
LAST = FULL_TILES
REST_FEATS = ATOM_FEATS - FULL_TILES * K_PASS
COPY_SHIFT = (ATOM_FEATS - ONCE_FEATS) // BLOCK

PAIR_TILES = PAIRS // P
PARTNERS = ATOMS // PAIR_TILES
N_COLS = 512
COL_TILES = H // N_COLS

X_CHUNKS = P // SOURCES
X_TILES = FULL_TILES // X_CHUNKS

TILE_ORDER = tuple(range(1, FULL_TILES)) + (0, LAST)
EARLY_PAIR_TILES = PAIR_TILES - 1
Z_BONDS = PAIR_TILES * 2 * BOND_FEATS
Z_FEATS = Z_BONDS - 2 * BOND_FEATS + K_PASS


COPY_HIGH_BEFORE = 6


WARM_MATMULS = 4


PLANE_RUNS = ((2, 2), (4, 4))


def bank_name(v, c):
    return "bank%d" % (COL_TILES * v + c)


FLOPS = 2 * PAIRS * (2 * ATOM_FEATS - ONCE_FEATS + 2 * BOND_FEATS) * H


def tile_mpnencoder_pa_k_kernel(tc, f_atoms, f_bonds, adj, W_i_w_words, W_i_w_scales, out):
    nc = tc.nc
    word_rows = W_i_w_words.rearrange("g p n -> (g p) n")
    scale_rows = W_i_w_scales.rearrange("g q n -> (g q) n")
    out_rows = out.rearrange("b m n h -> (b m n) h").rearrange("(j v) h -> v j h", v=PAIR_TILES)

    with ExitStack() as ctx:
        ctx.enter_context(tc.manual_schedule())
        keep = ctx.enter_context(tc.tile_pool(name="keep", bufs=1))
        stage = ctx.enter_context(tc.tile_pool(name="stage", bufs=3))
        results = ctx.enter_context(tc.tile_pool(name="results", bufs=4))
        psum = ctx.enter_context(tc.psum_pool(name="psum", bufs=1))

        both_words = {}
        for i in range(1, FULL_TILES):
            both_words[i] = keep.tile([P, 2, 2 * H], U8, align_bytes=64, name="both_words%d" % i)
        zero_words = keep.tile([P, 2 * H], U8, align_bytes=64)
        last_words = keep.tile([P, 2 * H], U8, align_bytes=64)
        opening = TILE_ORDER[0]
        opening_planes = keep.tile([P, 2, H], U8, align_bytes=64)
        first_runs = {}
        second_runs = {}
        run_of = {}
        for begin, count in PLANE_RUNS:
            first_runs[begin] = keep.tile([P, count, H], U8, align_bytes=64, name="first_planes%d" % begin)
            second_runs[begin] = keep.tile([P, count, H], U8, align_bytes=64, name="second_planes%d" % begin)
            for k in range(count):
                run_of[begin + k] = begin
        zero_plane = keep.tile([P, 1, H], U8, align_bytes=64)
        last_plane = keep.tile([P, H], U8, align_bytes=64)
        g_codes = keep.tile([P, FULL_TILES + 1, PAIRS], U32, align_bytes=64)
        g_planes = keep.tile([P, FULL_TILES + 1, PAIRS], U8, align_bytes=64)

        identity = keep.tile([P, P], F32)
        warm = keep.tile([P, N_COLS], BF16)
        ones = keep.tile([P, P], BF16)
        adj_row = keep.tile([P, PAIRS], BF16)
        adj_x4 = {}
        for v in range(PAIR_TILES):
            adj_x4[v] = keep.tile([P, P, PACK], BF16, name="adj_x4_%d" % v)
        x_sb = keep.tile([P, X_TILES * K_PASS], BF16)
        atoms_t = keep.tile([P, FULL_TILES, SOURCES, PACK], BF16)
        atoms_last = keep.tile([P, SOURCES, PACK], BF16)
        bonds_t = keep.tile([2 * BLOCK_PARTS, PAIRS, PACK], BF16)
        z_raw = keep.tile([P, PAIR_TILES * BOND_FEATS], BF16)
        z_sb = keep.tile([P, Z_FEATS], BF16)

        nc.vector.memset(warm[:].bitcast(I32), 0)
        warm_ps = psum.tile([P, N_COLS], F32, tag=bank_name(0, 0))
        for number in range(WARM_MATMULS):
            nc.tensor.matmul(out=warm_ps[:], lhsT=warm[:, 0:P], rhs=warm[:], start=True, stop=True)

        nc.gpsimd.memset(adj_row[:].bitcast(F32), 0.0)
        nc.gpsimd.memset(z_sb[:, Z_BONDS:Z_FEATS].bitcast(F32), 0.0)
        nc.gpsimd.memset(ones[:], 1.0)
        make_identity(nc, identity[:])
        nc.gpsimd.memset(atoms_last[:], 0.0)
        nc.gpsimd.memset(second_runs[4][:].bitcast(F32), 0.0)
        nc.gpsimd.memset(zero_plane[:].bitcast(F32), 0.0)
        nc.gpsimd.memset(last_plane[:].bitcast(F32), 0.0)

        nc.scalar.dma_start(
            out=z_raw[:],
            in_=f_bonds.rearrange("b m n f -> (b m n) f").rearrange("(j v) f -> j (v f)", v=PAIR_TILES),
        )

        first_l = TILE_ORDER[0] % X_TILES
        nc.sync.dma_start(
            out=x_sb[:],
            in_=f_atoms[:, :, 0 : FULL_TILES * K_PASS].rearrange("b m (c j) -> (b m) c j", c=X_CHUNKS),
        )
        nc.sync.dma_start(out=adj_row[0:1, :], in_=adj.rearrange("b m n -> (b m n)").unsqueeze(0))

        def load_words(words, first_block, blocks, first_part):
            nc.sync.dma_start(
                out=words[first_part : first_part + BLOCK_PARTS * blocks, :].bitcast(I32),
                in_=word_rows[BLOCK_PARTS * first_block : BLOCK_PARTS * (first_block + blocks), :].bitcast(I32),
            )

        def both_copies(rows, per_block):
            length = COPY_SHIFT * per_block
            begin = rows.shape[0] - 2 * length
            return rows[begin:, :].rearrange("(e x) n -> e x n", e=2), begin // per_block

        def load_tile_words(i):
            if i == 0:
                load_words(zero_words[:], 0, PASS_BLOCKS, 0)
                return
            view, block0 = both_copies(word_rows.bitcast(I32), BLOCK_PARTS)
            first = BLOCK_PARTS * (PASS_BLOCKS * i - block0)
            nc.sync.dma_start(
                out=both_words[i][:].bitcast(I32), in_=view[:, first : first + P, :].rearrange("e p n -> p e n")
            )

        def load_opening_planes():
            view, block0 = both_copies(scale_rows.bitcast(I32), 1)
            first = PASS_BLOCKS * opening - block0
            rows = view[:, first : first + PASS_BLOCKS, :].rearrange("e (q s) n -> s q e n", s=4)
            for s in range(4):
                nc.sync.dma_start(out=opening_planes[s:P:32, :, :].bitcast(I32), in_=rows[s])

        def load_planes(planes, first_block):
            count = planes.shape[1]
            rows = scale_rows[first_block : first_block + PASS_BLOCKS * count, :].rearrange(
                "(i q s) n -> s q i n", q=4, s=4
            )
            for s in range(4):
                nc.sync.dma_start(out=planes[s:P:32, :, :].bitcast(I32), in_=rows[s].bitcast(I32))

        def load_last_tile():
            rest_blocks = REST_FEATS // BLOCK
            once_blocks = ONCE_FEATS // BLOCK
            atom_blocks = ATOM_FEATS // BLOCK
            bond_run = (0, atom_blocks + COPY_SHIFT, 2)
            rest_first_run = (2, FULL_TILES * PASS_BLOCKS, rest_blocks)
            rest_second_run = (2 + rest_blocks, FULL_TILES * PASS_BLOCKS + COPY_SHIFT, rest_blocks)
            low_second_run = (once_blocks, atom_blocks, PASS_BLOCKS - once_blocks)
            for position, first_block, blocks in (bond_run, rest_first_run, rest_second_run, low_second_run):
                load_words(last_words[:], first_block, blocks, BLOCK_PARTS * position)
                done = 0
                while done < blocks:
                    q = position + done
                    step = min(4 - q % 4, blocks - done)
                    part = 32 * (q // 4) + q % 4
                    nc.sync.dma_start(
                        out=last_plane[part : part + step, :].bitcast(I32),
                        in_=scale_rows[first_block + done : first_block + done + step, :].bitcast(I32),
                    )
                    done += step

        load_tile_words(opening)
        nc.vector.memset(opening_planes[:].bitcast(I32), 0)
        load_opening_planes()
        load_tile_words(2)
        nc.vector.memset(first_runs[2][:].bitcast(I32), 0)
        load_planes(first_runs[2][:], PASS_BLOCKS * 2)
        nc.vector.memset(second_runs[2][:].bitcast(I32), 0)
        load_planes(second_runs[2][:], PASS_BLOCKS * 2 + COPY_SHIFT)
        load_tile_words(3)
        load_tile_words(4)
        nc.vector.memset(first_runs[4][:].bitcast(I32), 0)
        load_planes(first_runs[4][:], PASS_BLOCKS * 4)
        load_planes(second_runs[4][:], PASS_BLOCKS * 4 + COPY_SHIFT)
        load_tile_words(5)

        def late_loads():
            rest_parts = REST_FEATS // PACK
            rest_view = f_atoms[:, :, FULL_TILES * K_PASS : ATOM_FEATS].rearrange("b m (p t) -> p (b m) t", t=PACK)
            for copy in range(2):
                first = 2 * BLOCK_PARTS + rest_parts * copy
                nc.sync.dma_start(out=atoms_last[first : first + rest_parts, :, :], in_=rest_view)
            load_tile_words(6)
            load_tile_words(7)
            load_planes(zero_plane[:], 0)
            load_tile_words(0)
            load_last_tile()

        nc.scalar.copy(
            out=z_sb[:, 0:Z_BONDS].rearrange("j (v c f) -> j v c f", c=2, f=BOND_FEATS),
            in_=z_raw[:]
            .rearrange("j (v f) -> j v f", f=BOND_FEATS)
            .unsqueeze(2)
            .to_broadcast([P, PAIR_TILES, 2, BOND_FEATS]),
        )

        head_ps = psum.tile([P, 3, P], F32, tag=bank_name(2, 0))
        adj_ps = psum.tile([P, PAIRS], F32, tag=bank_name(2, 1))
        other_ps = psum.tile([P, 2, P], F32, tag=bank_name(1, 1))
        xt = {first_l: head_ps, 1 - first_l: other_ps}

        def transpose_atoms(l):
            x_words = x_sb[:, K_PASS * l : K_PASS * (l + 1)].bitcast(F32)
            for u in range(2):
                nc.tensor.transpose(xt[l][:, u, :], x_words[:, u : K_PASS // 2 : 2], identity[:])

        transpose_atoms(first_l)
        nc.tensor.matmul(
            out=head_ps[:, 2, :], lhsT=ones[:], rhs=adj_row[:, 0:PAIRS:PAIR_TILES], start=True, stop=True
        )
        nc.tensor.matmul(out=adj_ps[:], lhsT=ones[:], rhs=adj_row[:], start=True, stop=True)
        transpose_atoms(1 - first_l)
        z_words = z_sb[:].bitcast(F32)
        slabs_per_bank = N_COLS // (2 * P)
        zt = {}
        for half in range(PAIR_TILES // slabs_per_bank):
            zt[half] = psum.tile(
                [P, slabs_per_bank, 2, P], F32, name="zt%d" % half, tag=bank_name(EARLY_PAIR_TILES, half)
            )
            for s in range(slabs_per_bank):
                first = BOND_FEATS * (slabs_per_bank * half + s)
                for u in range(2):
                    nc.tensor.transpose(
                        zt[half][:, s, u, :], z_words[:, first + u : first + K_PASS // 2 : 2], identity[:]
                    )

        atoms_words = atoms_t[:].bitcast(F32)
        bonds_words = bonds_t[:].bitcast(F32)

        def gate(i, v, adj_of_pairs):
            grouped = stage.tile([P, P, PACK], BF16, align_bytes=64, name="grouped")
            nc.vector.tensor_tensor(
                out=grouped[:].rearrange("p (a k) t -> p a k t", k=PARTNERS),
                in0=(atoms_last[:] if i == LAST else atoms_t[:, i, :, :])
                .unsqueeze(2)
                .to_broadcast([P, SOURCES, PARTNERS, PACK]),
                in1=adj_of_pairs,
                op=MULT,
            )
            if i == LAST:
                bond_parts = slice(0, 2 * BLOCK_PARTS)
                nc.vector.tensor_tensor(
                    out=grouped[bond_parts, :, :],
                    in0=bonds_t[:, P * v : P * (v + 1), :],
                    in1=adj_x4[v][bond_parts, :, :],
                    op=MULT,
                )
            return grouped

        def gate_from_sbuf(i, v):
            return gate(i, v, adj_x4[v][:].rearrange("p (a k) t -> p a k t", k=PARTNERS))

        def quantise(i, v, grouped):
            pairs = slice(P * v, P * (v + 1))
            nc.vector.quantize_mx(
                out=g_codes[:, i, pairs].bitcast(FP8X4),
                scales=g_planes[:, i, pairs],
                in_=grouped[:].rearrange("p w t -> p (w t)"),
            )

        first_tile = TILE_ORDER[0]
        first_chunk = first_tile // X_TILES
        by_chunk = head_ps[:, 0:2, :].rearrange("p u (a c) -> p c a u", c=X_CHUNKS)
        nc.vector.tensor_copy(out=atoms_words[:, first_tile, :, :], in_=by_chunk[:, first_chunk, :, :])
        gated = gate(
            first_tile,
            0,
            head_ps[:, 2, :]
            .rearrange("p (a k) -> p a k", k=PARTNERS)
            .unsqueeze(3)
            .to_broadcast([P, SOURCES, PARTNERS, PACK]),
        )
        nc.vector.tensor_copy(
            out=atoms_words[:, first_tile + X_TILES : FULL_TILES : X_TILES, :, :],
            in_=by_chunk[:, first_chunk + 1 : X_CHUNKS, :, :],
        )

        def spread_adj(v):
            nc.scalar.copy(
                out=adj_x4[v][:],
                in_=adj_ps[:, v:PAIRS:PAIR_TILES].unsqueeze(2).to_broadcast([P, P, PACK]),
            )

        spread_adj(1)
        spread_adj(2)
        spread_adj(0)
        nc.scalar.copy(
            out=atoms_words[:, 1 - first_l : FULL_TILES : X_TILES, :, :],
            in_=other_ps[:].rearrange("p u (a c) -> p c a u", c=X_CHUNKS),
        )
        spread_adj(3)
        bond_parts = slice(0, 2 * BLOCK_PARTS)
        for half in range(PAIR_TILES // slabs_per_bank):
            nc.scalar.copy(
                out=bonds_words[:, slabs_per_bank * P * half : slabs_per_bank * P * (half + 1), :].rearrange(
                    "p (s j) u -> p s j u", j=P
                ),
                in_=zt[half][bond_parts, :, :, :].rearrange("p s u j -> p s j u"),
            )

        partners = []
        partners.append([(zero_words[:], zero_plane[:, 0, :])])
        for i in range(1, FULL_TILES):
            if i == opening:
                planes = (opening_planes[:, 0, :], opening_planes[:, 1, :])
            else:
                begin = run_of[i]
                planes = (first_runs[begin][:, i - begin, :], second_runs[begin][:, i - begin, :])
            partners.append([(both_words[i][:, 0, :], planes[0]), (both_words[i][:, 1, :], planes[1])])
        partners.append([(last_words[:], last_plane[:])])

        banks = {}

        def open_banks(v):
            for c in range(COL_TILES):
                banks[(v, c)] = psum.tile([P, N_COLS], F32, name=bank_name(v, c), tag=bank_name(v, c))

        def mx_passes(i, v, c):
            pairs = slice(P * v, P * (v + 1))
            for number, (words, plane) in enumerate(partners[i]):
                nc.tensor.matmul_mx(
                    out=banks[(v, c)][:],
                    lhsT=g_codes[:, i, pairs].bitcast(FP8X4),
                    lhsT_scale=g_planes[:, i, pairs],
                    rhs=words[:, 2 * N_COLS * c : 2 * N_COLS * (c + 1)].bitcast(FP4X4),
                    rhs_scale=plane[:, N_COLS * c : N_COLS * (c + 1)],
                    start=(i == TILE_ORDER[0] and number == 0),
                    stop=(i == TILE_ORDER[-1]),
                )

        def store_bank(v, c):
            if (v, c) == (PAIR_TILES - 1, COL_TILES - 1):
                for half, queue in enumerate((nc.sync, nc.scalar)):
                    cols = slice(N_COLS // 2 * half, N_COLS // 2 * (half + 1))
                    half_result = results.tile([P, N_COLS // 2], F32, name="half_result")
                    nc.vector.tensor_copy(out=half_result[:], in_=banks[(v, c)][:, cols])
                    queue.dma_start(
                        out=out_rows[v][:, N_COLS * c + cols.start : N_COLS * c + cols.stop], in_=half_result[:]
                    )
                return
            result = results.tile([P, N_COLS], F32, name="result")
            if c % 2 == 0:
                nc.scalar.copy(out=result[:], in_=banks[(v, c)][:])
            else:
                nc.vector.tensor_copy(out=result[:], in_=banks[(v, c)][:])
            nc.sync.dma_start(out=out_rows[v][:, N_COLS * c : N_COLS * (c + 1)], in_=result[:])

        for v in range(EARLY_PAIR_TILES):
            open_banks(v)
        steps = [(i, v) for i in TILE_ORDER for v in range(EARLY_PAIR_TILES)]
        steps.extend([(i, v) for v in range(EARLY_PAIR_TILES, PAIR_TILES) for i in TILE_ORDER])
        for index, (i, v) in enumerate(steps):
            if index == COPY_HIGH_BEFORE:
                high = slice(P // 2, P)
                nc.vector.tensor_copy(out=atoms_last[high, :, :], in_=atoms_t[high, 0, :, :])
                late_loads()
            ready = gated
            if 0 < index < len(steps) - 1:
                gated = gate_from_sbuf(*steps[index + 1])
            quantise(i, v, ready)
            if index == 0:
                gated = gate_from_sbuf(*steps[1])
            if v < EARLY_PAIR_TILES:
                for c in range(COL_TILES):
                    mx_passes(i, v, c)

        for v in range(EARLY_PAIR_TILES):
            for c in range(COL_TILES):
                store_bank(v, c)
        for v in range(EARLY_PAIR_TILES, PAIR_TILES):
            open_banks(v)
            for c in range(COL_TILES):
                for i in TILE_ORDER:
                    mx_passes(i, v, c)
                store_bank(v, c)
